import numpy as np
import ml_dtypes


def mxq(x, axis, fmt="e4m3"):
    dtype, down = {"e4m3": (ml_dtypes.float8_e4m3fn, 7), "e5m2": (ml_dtypes.float8_e5m2, 14)}[fmt]
    v = np.moveaxis(np.asarray(x, np.float32).astype(ml_dtypes.bfloat16).astype(np.float64), axis, -1)
    blocks = v.reshape(v.shape[:-1] + (-1, 32))
    amax = np.abs(blocks).max(-1, keepdims=True)
    byte = np.maximum(np.where(amax > 0, np.frexp(amax)[1] - 1 + 127, 0) - down, 1)
    scale = np.exp2(byte - 127.0)
    codes = (blocks / scale).astype(np.float32).astype(dtype).astype(np.float64)
    return np.moveaxis((codes * scale).reshape(v.shape), -1, axis)


WIDE = False


def mx_kscale(k):
    if not WIDE:
        return np.ones(k)
    levels = np.array([10, -10, 5, -5, 0])
    a = np.random.permutation(np.resize(levels, k // 512 * 4)).reshape(k // 512, 4)
    idx = np.arange(k)
    return np.exp2(a[idx // 512, idx % 128 // 32])


BF16 = ml_dtypes.bfloat16


def bf(x):
    return np.asarray(x, np.float32).astype(BF16)


def f64(x):
    return np.asarray(x).astype(np.float64)


B, F, N, D, HID, CELL, BUF = 512, 8, 8, 64, 128, 512, 512


def erf(v):
    a = np.minimum(np.abs(v), 6.0)
    a2 = a * a
    term = a.copy()
    total = a.copy()
    for n in range(1, 100):
        term = term * (a2 / (n + 0.5))
        total = total + term
    return np.sign(v) * (2.0 / np.sqrt(np.pi)) * np.exp(-a2) * total


def gelu(v):
    return 0.5 * v * (1.0 + erf(v / np.sqrt(2.0)))


def elu(v):
    return np.where(v > 0.0, v, np.exp(np.minimum(v, 0.0)) - 1.0)


def setup_inputs():
    s = mx_kscale(D * F)
    c = mx_kscale(CELL)
    zs = s.reshape(D, F).T[None, :, None, :]
    rows = np.concatenate([c, np.ones(BUF)])
    return {"z": bf(np.random.standard_normal((B, F, N, D)) * zs),
            "cells": bf(np.random.standard_normal((B, N, CELL)) * c),
            "buf_W": bf(np.random.standard_normal((F * D, BUF)) / np.sqrt(F * D) / s[:, None]),
            "buf_b": bf(np.random.standard_normal(BUF) * 0.3),
            "lam_W1": bf(np.random.standard_normal((CELL + BUF, HID)) / np.sqrt(CELL + BUF) / rows[:, None]),
            "lam_b1": bf(np.random.standard_normal(HID) * 0.3)}


def reference(z, cells, buf_W, buf_b, lam_W1, lam_b1):
    zt = f64(z).transpose(0, 2, 3, 1).reshape(B, N, D * F)
    z_b = elu((mxq(zt, 2, "e4m3") @ mxq(f64(buf_W), 0, "e4m3")) + f64(buf_b))
    w = f64(lam_W1)
    p = mxq(f64(cells), 2, "e4m3") @ mxq(w[:CELL], 0, "e4m3")
    q = mxq(z_b, 2, "e4m3") @ mxq(w[CELL:], 0, "e4m3")
    return gelu(p[:, :, None, :] + q[:, None, :, :] + f64(lam_b1))

@@ -1,0 +1,252 @@
+import concourse.masks as masks
+import concourse.mybir as mybir
+
+F32 = mybir.dt.float32
+BF16 = mybir.dt.bfloat16
+U32 = mybir.dt.uint32
+U8 = mybir.dt.uint8
+FP8X4 = mybir.dt.float8_e4m3fn_x4
+ACT = mybir.ActivationFunctionType
+ALU = mybir.AluOpType
+
+P = 128
+BATCH, FRAMES, SLOTS, FEAT, HID, CELL, BUF = 512, 8, 8, 64, 128, 512, 512
+PACK = 4
+K = P * PACK
+WORDS = K // 2
+B_TILES = BATCH // P
+GROUP_SLOTS = 4
+GROUP_TOKENS = GROUP_SLOTS * P
+GROUPS = B_TILES * SLOTS // GROUP_SLOTS
+OUT_BLOCKS = BUF // P
+PAIR_ROWS = 2
+HALF = SLOTS // 2
+
+FLOPS = 2 * BATCH * SLOTS * K * (BUF + HID + HID)
+
+
+def tile_interaction_net_pa_t_kernel(tc, z, cells, buf_W, buf_b, lam_W1, lam_b1, out):
+    nc = tc.nc
+
+    def live(g):
+        return 0 <= g < GROUPS
+
+    with tc.manual_schedule(), tc.tile_pool(name="keep", bufs=1) as keep:
+        w_codes = keep.tile([P, BUF], U32, align_bytes=64)
+        w_scales = keep.tile([P, BUF], U8, align_bytes=64)
+        l_codes = keep.tile([P, 2 * HID], U32, align_bytes=64)
+        l_scales = keep.tile([P, 2 * HID], U8, align_bytes=64)
+        c_codes = keep.tile([P, GROUPS * GROUP_TOKENS], U32, align_bytes=64)
+        c_scales = keep.tile([P, GROUPS * GROUP_TOKENS], U8, align_bytes=64)
+        zb_codes = keep.tile([P, GROUPS * GROUP_TOKENS], U32, align_bytes=64)
+        zb_scales = keep.tile([P, GROUPS * GROUP_TOKENS], U8, align_bytes=64)
+        buf_bias = keep.tile([P, OUT_BLOCKS], F32)
+        lam_bias = keep.tile([P, HID], BF16)
+
+        with (
+            tc.tile_pool(name="inputs", bufs=1) as inputs,
+            tc.tile_pool(name="stage", bufs=2) as stage,
+            tc.psum_pool(name="flip", bufs=4) as flip,
+            tc.psum_pool(name="mm1", bufs=OUT_BLOCKS) as mm1,
+        ):
+            bias_rows = inputs.tile([P, P], BF16)
+            nc.vector.memset(bias_rows[:], 0.0)
+            w_raw = inputs.tile([P, PACK, BUF], BF16)
+            w_rows = buf_W.rearrange("(d2 t fl) o -> fl d2 t o", t=PACK, fl=4)
+            for fl in range(4):
+                nc.sync.dma_start(out=w_raw[fl:P:4, :, :], in_=w_rows[fl])
+            l_raw = inputs.tile([P, 2, PACK, HID], BF16)
+            nc.sync.dma_start(
+                out=l_raw[:, 0].rearrange("q (u e) h -> q u (e h)", u=2),
+                in_=lam_W1[0:K, :].rearrange("(u q e) h -> q u (e h)", u=2, e=2),
+            )
+            nc.sync.dma_start(out=l_raw[:, 1], in_=lam_W1[K : 2 * K, :].rearrange("(t q) h -> q t h", t=PACK))
+            z_raw = []
+            c_raw = []
+            for bt in range(B_TILES):
+                rows = slice(bt * P, (bt + 1) * P)
+                z_in = inputs.tile([P, SLOTS * K], BF16, name="z_in%d" % bt)
+                nc.sync.dma_start(out=z_in[:], in_=z[rows].rearrange("b f n d -> b (f n d)"))
+                z_raw.append(z_in)
+                if bt == 0:
+                    nc.sync.dma_start(out=bias_rows[0:OUT_BLOCKS, :], in_=buf_b.rearrange("(t q) -> t q", q=P))
+                c_in = inputs.tile([P, SLOTS * K], BF16, name="c_in%d" % bt)
+                nc.sync.dma_start(out=c_in[:], in_=cells[rows].rearrange("b n k -> b (n k)"))
+                c_raw.append(c_in)
+                if bt == 0:
+                    nc.sync.dma_start(out=lam_bias[:], in_=lam_b1.partition_broadcast(P))
+
+            ident_f32 = inputs.tile([P, P], F32)
+            masks.make_identity(nc, ident_f32[:])
+            ident_bf16 = inputs.tile([P, P], BF16)
+            masks.make_identity(nc, ident_bf16[:])
+
+            w_grouped = inputs.tile([P, BUF * PACK], BF16, align_bytes=64)
+            nc.vector.tensor_copy(
+                out=w_grouped[:].rearrange("q (o u e) -> q o u e", u=2, e=2),
+                in_=w_raw[:].rearrange("q (e u) o -> q o u e", e=2),
+            )
+            l_grouped = inputs.tile([P, 2 * HID * PACK], BF16, align_bytes=64)
+            nc.vector.tensor_copy(
+                out=l_grouped[:].rearrange("q (w h t) -> q w h t", w=2, t=PACK),
+                in_=l_raw[:].rearrange("q w t h -> q w h t"),
+            )
+            nc.vector.quantize_mx(out=w_codes[:].bitcast(FP8X4), scales=w_scales[:], in_=w_grouped[:])
+            nc.vector.quantize_mx(out=l_codes[:].bitcast(FP8X4), scales=l_scales[:], in_=l_grouped[:])
+            bias_cols = flip.tile([P, P], BF16, tag="bank")
+            nc.tensor.transpose(out=bias_cols[:], in_=bias_rows[:], identity=ident_bf16[:])
+            nc.vector.tensor_copy(out=buf_bias[:], in_=bias_cols[:, 0:OUT_BLOCKS])
+
+            z_sorted, z_banks, z_grouped, z_codes, z_scales = {}, {}, {}, {}, {}
+            c_banks, c_grouped = {}, {}
+            exps, relus, zb_grouped = {}, {}, {}
+
+            def sort_z(g):
+                bt, half = divmod(g, 2)
+                words = stage.tile([P, GROUP_SLOTS * WORDS], F32, name="z_sorted", bufs=3)
+                source = z_raw[bt][:].bitcast(F32).rearrange(
+                    "b (u fl n d2) -> b n u d2 fl", u=2, fl=4, n=SLOTS
+                )
+                nc.vector.tensor_copy(
+                    out=words[:].rearrange("b (n u d2 fl) -> b n u d2 fl", n=GROUP_SLOTS, u=2, fl=4),
+                    in_=source[:, half * GROUP_SLOTS : (half + 1) * GROUP_SLOTS],
+                )
+                z_sorted[g] = words[:]
+
+            def flip_words(words):
+                banks = []
+                for pair in range(2):
+                    bank = flip.tile([P, 2, 2, P], F32, tag="bank")
+                    for n in range(2):
+                        for u in range(2):
+                            first = ((2 * pair + n) * 2 + u) * P
+                            nc.tensor.transpose(
+                                out=bank[:, n, u, :], in_=words[:, first : first + P], identity=ident_f32[:]
+                            )
+                    banks.append(bank)
+                return banks
+
+            def interleave(copy, banks, name):
+                grouped = stage.tile([P, GROUP_TOKENS * PACK], BF16, name=name, align_bytes=64)
+                words = grouped[:].bitcast(F32).rearrange("q (n b u) -> q n b u", n=GROUP_SLOTS, u=2)
+                for pair in range(2):
+                    copy(out=words[:, 2 * pair : 2 * pair + 2], in_=banks[pair][:].rearrange("q n u b -> q n b u"))
+                return grouped
+
+            def quantise_z(g):
+                codes = stage.tile([P, GROUP_TOKENS], U32, name="z_codes", align_bytes=64)
+                scales = stage.tile([P, GROUP_TOKENS], U8, name="z_scales", align_bytes=64)
+                nc.vector.quantize_mx(out=codes[:].bitcast(FP8X4), scales=scales[:], in_=z_grouped[g][:])
+                z_codes[g], z_scales[g] = codes, scales
+
+            def buffer_layer(g):
+                exp_v = stage.tile([P, OUT_BLOCKS, GROUP_TOKENS], F32, name="exp_v")
+                relu_v = stage.tile([P, OUT_BLOCKS, GROUP_TOKENS], F32, name="relu_v")
+                for t in range(OUT_BLOCKS):
+                    acc = mm1.tile([P, GROUP_TOKENS], F32, name="acc")
+                    nc.tensor.matmul_mx(
+                        out=acc[:],
+                        lhsT=w_codes[:, t * P : (t + 1) * P].bitcast(FP8X4),
+                        lhsT_scale=w_scales[:, t * P : (t + 1) * P],
+                        rhs=z_codes[g][:].bitcast(FP8X4),
+                        rhs_scale=z_scales[g][:],
+                        start=True,
+                        stop=True,
+                    )
+                    nc.scalar.activation(out=exp_v[:, t, :], in_=acc[:], func=ACT.Exp, bias=buf_bias[:, t : t + 1])
+                    nc.scalar.activation(out=relu_v[:, t, :], in_=acc[:], func=ACT.Relu, bias=buf_bias[:, t : t + 1])
+                exps[g], relus[g] = exp_v, relu_v
+
+            def combine(g):
+                grouped = stage.tile([P, GROUP_TOKENS * PACK], BF16, name="zb_grouped", align_bytes=64)
+                nc.vector.scalar_tensor_tensor(
+                    out=grouped[:].rearrange("q (r t) -> q r t", t=PACK),
+                    in0=exps[g][:].rearrange("q t r -> q r t"),
+                    scalar=-1.0,
+                    in1=relus[g][:].rearrange("q t r -> q r t"),
+                    op0=ALU.add,
+                    op1=ALU.min,
+                )
+                zb_grouped[g] = grouped
+
+            def quantise_into(codes, scales, g, grouped):
+                cols = slice(g * GROUP_TOKENS, (g + 1) * GROUP_TOKENS)
+                nc.vector.quantize_mx(out=codes[:, cols].bitcast(FP8X4), scales=scales[:, cols], in_=grouped[:])
+
+            for k in range(-2, GROUPS + 1):
+                if live(k - 1):
+                    combine(k - 1)
+                if live(k):
+                    buffer_layer(k)
+                if live(k + 1):
+                    z_banks[k + 1] = flip_words(z_sorted[k + 1])
+                    z_grouped[k + 1] = interleave(nc.vector.tensor_copy, z_banks[k + 1], "z_grouped")
+                if live(k - 1):
+                    quantise_into(zb_codes, zb_scales, k - 1, zb_grouped[k - 1])
+                if live(k + 1):
+                    bt, half = divmod(k + 1, 2)
+                    c_words = c_raw[bt][:].bitcast(F32)[:, half * GROUP_SLOTS * WORDS : (half + 1) * GROUP_SLOTS * WORDS]
+                    c_banks[k + 1] = flip_words(c_words)
+                    c_grouped[k + 1] = interleave(nc.scalar.copy, c_banks[k + 1], "c_grouped")
+                if live(k + 2):
+                    sort_z(k + 2)
+                if live(k + 1):
+                    quantise_z(k + 1)
+                if live(k):
+                    quantise_into(c_codes, c_scales, k, c_grouped[k])
+
+        with (
+            tc.tile_pool(name="sums", bufs=2) as sums,
+            tc.tile_pool(name="chunks", bufs=4) as chunks,
+            tc.psum_pool(name="proj", bufs=2) as proj,
+        ):
+            p_biased, q_banks = {}, {}
+
+            def project(codes, scales, weight, bt, half, name, bufs):
+                bank = proj.tile([P, HALF, HID], F32, name=name, bufs=bufs)
+                for s in range(HALF):
+                    first = (bt * SLOTS + half * HALF + s) * P
+                    nc.tensor.matmul_mx(
+                        out=bank[:, s, :],
+                        lhsT=codes[:, first : first + P].bitcast(FP8X4),
+                        lhsT_scale=scales[:, first : first + P],
+                        rhs=l_codes[:, weight * HID : (weight + 1) * HID].bitcast(FP8X4),
+                        rhs_scale=l_scales[:, weight * HID : (weight + 1) * HID],
+                        start=True,
+                        stop=True,
+                    )
+                return bank
+
+            def project_tile(bt):
+                p_sb = sums.tile([P, SLOTS, HID], F32, name="p_sb")
+                for half in range(2):
+                    p_bank = project(c_codes, c_scales, 0, bt, half, "p_bank", 2)
+                    nc.vector.tensor_tensor(
+                        out=p_sb[:, half * HALF : (half + 1) * HALF, :],
+                        in0=p_bank[:],
+                        in1=lam_bias[:].unsqueeze(1).to_broadcast([P, HALF, HID]),
+                        op=ALU.add,
+                    )
+                p_biased[bt] = p_sb
+                q_banks[bt] = [project(zb_codes, zb_scales, 1, bt, half, "q_bank", 4) for half in range(2)]
+
+            project_tile(0)
+            for bt in range(B_TILES):
+                for first_i in range(0, SLOTS, PAIR_ROWS):
+                    if first_i == SLOTS - PAIR_ROWS and bt + 1 < B_TILES:
+                        project_tile(bt + 1)
+                    chunk = chunks.tile([P, PAIR_ROWS, SLOTS, HID], F32, name="chunk")
+                    for half in range(2):
+                        nc.vector.tensor_tensor(
+                            out=chunk[:, :, half * HALF : (half + 1) * HALF, :],
+                            in0=p_biased[bt][:, first_i : first_i + PAIR_ROWS, :]
+                            .unsqueeze(2)
+                            .to_broadcast([P, PAIR_ROWS, HALF, HID]),
+                            in1=q_banks[bt][half][:].unsqueeze(1).to_broadcast([P, PAIR_ROWS, HALF, HID]),
+                            op=ALU.add,
+                        )
+                    nc.scalar.activation(out=chunk[:], in_=chunk[:], func=ACT.Gelu)
+                    nc.sync.dma_start(
+                        out=out[bt * P : (bt + 1) * P, first_i : first_i + PAIR_ROWS].rearrange("b i j h -> b (i j h)"),
+                        in_=chunk[:].rearrange("b i j h -> b (i j h)"),
+                    )

@@ -19,8 +19,14 @@ GROUP_SLOTS = 4
 GROUP_TOKENS = GROUP_SLOTS * P
 GROUPS = B_TILES * SLOTS // GROUP_SLOTS
 OUT_BLOCKS = BUF // P
-PAIR_ROWS = 2
 HALF = SLOTS // 2
+CHUNK_ROWS = 2
+TILE_CHUNKS = SLOTS // CHUNK_ROWS
+CHUNKS = B_TILES * TILE_CHUNKS
+STEP_CHUNKS = 2
+POOL_SLOTS = 2
+FIRST_CHUNK_STEP = GROUPS - 1
+LAST_STEP = FIRST_CHUNK_STEP + CHUNKS // STEP_CHUNKS - 1
 
 FLOPS = 2 * BATCH * SLOTS * K * (BUF + HID + HID)
 
@@ -31,7 +37,12 @@ def tile_interaction_net_pa_t_kernel(tc, z, cells, buf_W, buf_b, lam_W1, lam_b1,
     def live(g):
         return 0 <= g < GROUPS
 
-    with tc.manual_schedule(), tc.tile_pool(name="keep", bufs=1) as keep:
+    with (
+        tc.manual_schedule(),
+        tc.tile_pool(name="keep", bufs=1) as keep,
+        tc.tile_pool(name="stage", bufs=2) as stage,
+        tc.psum_pool(name="psum", bufs=4) as psum,
+    ):
         w_codes = keep.tile([P, BUF], U32, align_bytes=64)
         w_scales = keep.tile([P, BUF], U8, align_bytes=64)
         l_codes = keep.tile([P, 2 * HID], U32, align_bytes=64)
@@ -43,210 +54,218 @@ def tile_interaction_net_pa_t_kernel(tc, z, cells, buf_W, buf_b, lam_W1, lam_b1,
         buf_bias = keep.tile([P, OUT_BLOCKS], F32)
         lam_bias = keep.tile([P, HID], BF16)
 
-        with (
-            tc.tile_pool(name="inputs", bufs=1) as inputs,
-            tc.tile_pool(name="stage", bufs=2) as stage,
-            tc.psum_pool(name="flip", bufs=4) as flip,
-            tc.psum_pool(name="mm1", bufs=OUT_BLOCKS) as mm1,
-        ):
-            bias_rows = inputs.tile([P, P], BF16)
-            nc.vector.memset(bias_rows[:], 0.0)
-            w_raw = inputs.tile([P, PACK, BUF], BF16)
-            w_rows = buf_W.rearrange("(d2 t fl) o -> fl d2 t o", t=PACK, fl=4)
-            for fl in range(4):
-                nc.sync.dma_start(out=w_raw[fl:P:4, :, :], in_=w_rows[fl])
-            l_raw = inputs.tile([P, 2, PACK, HID], BF16)
-            nc.sync.dma_start(
-                out=l_raw[:, 0].rearrange("q (u e) h -> q u (e h)", u=2),
-                in_=lam_W1[0:K, :].rearrange("(u q e) h -> q u (e h)", u=2, e=2),
-            )
-            nc.sync.dma_start(out=l_raw[:, 1], in_=lam_W1[K : 2 * K, :].rearrange("(t q) h -> q t h", t=PACK))
-            z_raw = []
-            c_raw = []
-            for bt in range(B_TILES):
-                rows = slice(bt * P, (bt + 1) * P)
-                z_in = inputs.tile([P, SLOTS * K], BF16, name="z_in%d" % bt)
-                nc.sync.dma_start(out=z_in[:], in_=z[rows].rearrange("b f n d -> b (f n d)"))
-                z_raw.append(z_in)
-                if bt == 0:
-                    nc.sync.dma_start(out=bias_rows[0:OUT_BLOCKS, :], in_=buf_b.rearrange("(t q) -> t q", q=P))
-                c_in = inputs.tile([P, SLOTS * K], BF16, name="c_in%d" % bt)
-                nc.sync.dma_start(out=c_in[:], in_=cells[rows].rearrange("b n k -> b (n k)"))
-                c_raw.append(c_in)
-                if bt == 0:
-                    nc.sync.dma_start(out=lam_bias[:], in_=lam_b1.partition_broadcast(P))
+        bias_rows = keep.tile([P, P], BF16)
+        nc.vector.memset(bias_rows[:], 0.0)
+        w_raw = keep.tile([P, PACK, BUF], BF16)
+        w_rows = buf_W.rearrange("(d2 t fl) o -> fl d2 t o", t=PACK, fl=4)
+        for fl in range(4):
+            nc.sync.dma_start(out=w_raw[fl:P:4, :, :], in_=w_rows[fl])
+        z_raw = [keep.tile([P, SLOTS * K], BF16, name="z_raw%d" % bt) for bt in range(B_TILES)]
+        c_raw = [keep.tile([P, SLOTS * K], BF16, name="c_raw%d" % bt) for bt in range(B_TILES)]
+        l_raw = keep.tile([P, 2, PACK, HID], BF16)
 
-            ident_f32 = inputs.tile([P, P], F32)
-            masks.make_identity(nc, ident_f32[:])
-            ident_bf16 = inputs.tile([P, P], BF16)
-            masks.make_identity(nc, ident_bf16[:])
+        def load_tile(bt):
+            rows = slice(bt * P, (bt + 1) * P)
+            nc.sync.dma_start(out=z_raw[bt][:], in_=z[rows].rearrange("b f n d -> b (f n d)"))
+            nc.sync.dma_start(out=c_raw[bt][:], in_=cells[rows].rearrange("b n k -> b (n k)"))
 
-            w_grouped = inputs.tile([P, BUF * PACK], BF16, align_bytes=64)
+        nc.sync.dma_start(out=bias_rows[0:OUT_BLOCKS, :], in_=buf_b.rearrange("(t q) -> t q", q=P))
+        load_tile(0)
+        nc.sync.dma_start(
+            out=l_raw[:, 0].rearrange("q (u e) h -> q u (e h)", u=2),
+            in_=lam_W1[0:K, :].rearrange("(u q e) h -> q u (e h)", u=2, e=2),
+        )
+        nc.sync.dma_start(out=l_raw[:, 1], in_=lam_W1[K : 2 * K, :].rearrange("(t q) h -> q t h", t=PACK))
+        nc.sync.dma_start(out=lam_bias[:], in_=lam_b1.partition_broadcast(P))
+        for bt in range(1, B_TILES):
+            load_tile(bt)
+
+        ident_f32 = keep.tile([P, P], F32)
+        masks.make_identity(nc, ident_f32[:])
+        ident_bf16 = keep.tile([P, P], BF16)
+        masks.make_identity(nc, ident_bf16[:])
+
+        z_sorted, z_grouped, z_codes, z_scales = {}, {}, {}, {}
+        c_grouped = {}
+        exps, relus, zb_grouped = {}, {}, {}
+
+        def sort_z(g):
+            bt, half = divmod(g, 2)
+            words = stage.tile([P, GROUP_SLOTS * WORDS], F32, name="z_sorted")
+            source = z_raw[bt][:].bitcast(F32).rearrange("b (u fl n d2) -> b n u d2 fl", u=2, fl=4, n=SLOTS)
             nc.vector.tensor_copy(
-                out=w_grouped[:].rearrange("q (o u e) -> q o u e", u=2, e=2),
-                in_=w_raw[:].rearrange("q (e u) o -> q o u e", e=2),
+                out=words[:].rearrange("b (n u d2 fl) -> b n u d2 fl", n=GROUP_SLOTS, u=2, fl=4),
+                in_=source[:, half * GROUP_SLOTS : (half + 1) * GROUP_SLOTS],
             )
-            l_grouped = inputs.tile([P, 2 * HID * PACK], BF16, align_bytes=64)
-            nc.vector.tensor_copy(
-                out=l_grouped[:].rearrange("q (w h t) -> q w h t", w=2, t=PACK),
-                in_=l_raw[:].rearrange("q w t h -> q w h t"),
-            )
-            nc.vector.quantize_mx(out=w_codes[:].bitcast(FP8X4), scales=w_scales[:], in_=w_grouped[:])
-            nc.vector.quantize_mx(out=l_codes[:].bitcast(FP8X4), scales=l_scales[:], in_=l_grouped[:])
-            bias_cols = flip.tile([P, P], BF16, tag="bank")
-            nc.tensor.transpose(out=bias_cols[:], in_=bias_rows[:], identity=ident_bf16[:])
-            nc.vector.tensor_copy(out=buf_bias[:], in_=bias_cols[:, 0:OUT_BLOCKS])
+            z_sorted[g] = words[:]
 
-            z_sorted, z_banks, z_grouped, z_codes, z_scales = {}, {}, {}, {}, {}
-            c_banks, c_grouped = {}, {}
-            exps, relus, zb_grouped = {}, {}, {}
-
-            def sort_z(g):
-                bt, half = divmod(g, 2)
-                words = stage.tile([P, GROUP_SLOTS * WORDS], F32, name="z_sorted", bufs=3)
-                source = z_raw[bt][:].bitcast(F32).rearrange(
-                    "b (u fl n d2) -> b n u d2 fl", u=2, fl=4, n=SLOTS
-                )
-                nc.vector.tensor_copy(
-                    out=words[:].rearrange("b (n u d2 fl) -> b n u d2 fl", n=GROUP_SLOTS, u=2, fl=4),
-                    in_=source[:, half * GROUP_SLOTS : (half + 1) * GROUP_SLOTS],
-                )
-                z_sorted[g] = words[:]
-
-            def flip_words(words):
-                banks = []
-                for pair in range(2):
-                    bank = flip.tile([P, 2, 2, P], F32, tag="bank")
-                    for n in range(2):
-                        for u in range(2):
-                            first = ((2 * pair + n) * 2 + u) * P
-                            nc.tensor.transpose(
-                                out=bank[:, n, u, :], in_=words[:, first : first + P], identity=ident_f32[:]
-                            )
-                    banks.append(bank)
-                return banks
-
-            def interleave(copy, banks, name):
-                grouped = stage.tile([P, GROUP_TOKENS * PACK], BF16, name=name, align_bytes=64)
-                words = grouped[:].bitcast(F32).rearrange("q (n b u) -> q n b u", n=GROUP_SLOTS, u=2)
-                for pair in range(2):
-                    copy(out=words[:, 2 * pair : 2 * pair + 2], in_=banks[pair][:].rearrange("q n u b -> q n b u"))
-                return grouped
-
-            def quantise_z(g):
-                codes = stage.tile([P, GROUP_TOKENS], U32, name="z_codes", align_bytes=64)
-                scales = stage.tile([P, GROUP_TOKENS], U8, name="z_scales", align_bytes=64)
-                nc.vector.quantize_mx(out=codes[:].bitcast(FP8X4), scales=scales[:], in_=z_grouped[g][:])
-                z_codes[g], z_scales[g] = codes, scales
-
-            def buffer_layer(g):
-                exp_v = stage.tile([P, OUT_BLOCKS, GROUP_TOKENS], F32, name="exp_v")
-                relu_v = stage.tile([P, OUT_BLOCKS, GROUP_TOKENS], F32, name="relu_v")
-                for t in range(OUT_BLOCKS):
-                    acc = mm1.tile([P, GROUP_TOKENS], F32, name="acc")
-                    nc.tensor.matmul_mx(
-                        out=acc[:],
-                        lhsT=w_codes[:, t * P : (t + 1) * P].bitcast(FP8X4),
-                        lhsT_scale=w_scales[:, t * P : (t + 1) * P],
-                        rhs=z_codes[g][:].bitcast(FP8X4),
-                        rhs_scale=z_scales[g][:],
-                        start=True,
-                        stop=True,
-                    )
-                    nc.scalar.activation(out=exp_v[:, t, :], in_=acc[:], func=ACT.Exp, bias=buf_bias[:, t : t + 1])
-                    nc.scalar.activation(out=relu_v[:, t, :], in_=acc[:], func=ACT.Relu, bias=buf_bias[:, t : t + 1])
-                exps[g], relus[g] = exp_v, relu_v
-
-            def combine(g):
-                grouped = stage.tile([P, GROUP_TOKENS * PACK], BF16, name="zb_grouped", align_bytes=64)
-                nc.vector.scalar_tensor_tensor(
-                    out=grouped[:].rearrange("q (r t) -> q r t", t=PACK),
-                    in0=exps[g][:].rearrange("q t r -> q r t"),
-                    scalar=-1.0,
-                    in1=relus[g][:].rearrange("q t r -> q r t"),
-                    op0=ALU.add,
-                    op1=ALU.min,
-                )
-                zb_grouped[g] = grouped
-
-            def quantise_into(codes, scales, g, grouped):
-                cols = slice(g * GROUP_TOKENS, (g + 1) * GROUP_TOKENS)
-                nc.vector.quantize_mx(out=codes[:, cols].bitcast(FP8X4), scales=scales[:, cols], in_=grouped[:])
-
-            for k in range(-2, GROUPS + 1):
-                if live(k - 1):
-                    combine(k - 1)
-                if live(k):
-                    buffer_layer(k)
-                if live(k + 1):
-                    z_banks[k + 1] = flip_words(z_sorted[k + 1])
-                    z_grouped[k + 1] = interleave(nc.vector.tensor_copy, z_banks[k + 1], "z_grouped")
-                if live(k - 1):
-                    quantise_into(zb_codes, zb_scales, k - 1, zb_grouped[k - 1])
-                if live(k + 1):
-                    bt, half = divmod(k + 1, 2)
-                    c_words = c_raw[bt][:].bitcast(F32)[:, half * GROUP_SLOTS * WORDS : (half + 1) * GROUP_SLOTS * WORDS]
-                    c_banks[k + 1] = flip_words(c_words)
-                    c_grouped[k + 1] = interleave(nc.scalar.copy, c_banks[k + 1], "c_grouped")
-                if live(k + 2):
-                    sort_z(k + 2)
-                if live(k + 1):
-                    quantise_z(k + 1)
-                if live(k):
-                    quantise_into(c_codes, c_scales, k, c_grouped[k])
-
-        with (
-            tc.tile_pool(name="sums", bufs=2) as sums,
-            tc.tile_pool(name="chunks", bufs=4) as chunks,
-            tc.psum_pool(name="proj", bufs=2) as proj,
-        ):
-            p_biased, q_banks = {}, {}
-
-            def project(codes, scales, weight, bt, half, name, bufs):
-                bank = proj.tile([P, HALF, HID], F32, name=name, bufs=bufs)
-                for s in range(HALF):
-                    first = (bt * SLOTS + half * HALF + s) * P
-                    nc.tensor.matmul_mx(
-                        out=bank[:, s, :],
-                        lhsT=codes[:, first : first + P].bitcast(FP8X4),
-                        lhsT_scale=scales[:, first : first + P],
-                        rhs=l_codes[:, weight * HID : (weight + 1) * HID].bitcast(FP8X4),
-                        rhs_scale=l_scales[:, weight * HID : (weight + 1) * HID],
-                        start=True,
-                        stop=True,
-                    )
-                return bank
-
-            def project_tile(bt):
-                p_sb = sums.tile([P, SLOTS, HID], F32, name="p_sb")
-                for half in range(2):
-                    p_bank = project(c_codes, c_scales, 0, bt, half, "p_bank", 2)
-                    nc.vector.tensor_tensor(
-                        out=p_sb[:, half * HALF : (half + 1) * HALF, :],
-                        in0=p_bank[:],
-                        in1=lam_bias[:].unsqueeze(1).to_broadcast([P, HALF, HID]),
-                        op=ALU.add,
-                    )
-                p_biased[bt] = p_sb
-                q_banks[bt] = [project(zb_codes, zb_scales, 1, bt, half, "q_bank", 4) for half in range(2)]
-
-            project_tile(0)
-            for bt in range(B_TILES):
-                for first_i in range(0, SLOTS, PAIR_ROWS):
-                    if first_i == SLOTS - PAIR_ROWS and bt + 1 < B_TILES:
-                        project_tile(bt + 1)
-                    chunk = chunks.tile([P, PAIR_ROWS, SLOTS, HID], F32, name="chunk")
-                    for half in range(2):
-                        nc.vector.tensor_tensor(
-                            out=chunk[:, :, half * HALF : (half + 1) * HALF, :],
-                            in0=p_biased[bt][:, first_i : first_i + PAIR_ROWS, :]
-                            .unsqueeze(2)
-                            .to_broadcast([P, PAIR_ROWS, HALF, HID]),
-                            in1=q_banks[bt][half][:].unsqueeze(1).to_broadcast([P, PAIR_ROWS, HALF, HID]),
-                            op=ALU.add,
+        def flip_and_interleave(words, copy, name):
+            grouped = stage.tile([P, GROUP_TOKENS * PACK], BF16, name=name, align_bytes=64)
+            pairs = grouped[:].bitcast(F32).rearrange("q (n b u) -> q n b u", n=GROUP_SLOTS, u=2)
+            banks = []
+            for pair in range(2):
+                bank = psum.tile([P, 2, 2, P], F32, tag="bank")
+                for n in range(2):
+                    for u in range(2):
+                        first = ((2 * pair + n) * 2 + u) * P
+                        nc.tensor.transpose(
+                            out=bank[:, n, u, :], in_=words[:, first : first + P], identity=ident_f32[:]
                         )
-                    nc.scalar.activation(out=chunk[:], in_=chunk[:], func=ACT.Gelu)
-                    nc.sync.dma_start(
-                        out=out[bt * P : (bt + 1) * P, first_i : first_i + PAIR_ROWS].rearrange("b i j h -> b (i j h)"),
-                        in_=chunk[:].rearrange("b i j h -> b (i j h)"),
-                    )
+                banks.append(bank)
+            for pair in range(2):
+                copy(out=pairs[:, 2 * pair : 2 * pair + 2], in_=banks[pair][:].rearrange("q n u b -> q n b u"))
+            return grouped
+
+        def quantise_z(g):
+            codes = stage.tile([P, GROUP_TOKENS], U32, name="z_codes", align_bytes=64)
+            scales = stage.tile([P, GROUP_TOKENS], U8, name="z_scales", align_bytes=64)
+            nc.vector.quantize_mx(out=codes[:].bitcast(FP8X4), scales=scales[:], in_=z_grouped[g][:])
+            z_codes[g], z_scales[g] = codes, scales
+
+        def buffer_layer(g):
+            exp_v = stage.tile([P, OUT_BLOCKS, GROUP_TOKENS], F32, tag="wide", bufs=4)
+            relu_v = stage.tile([P, OUT_BLOCKS, GROUP_TOKENS], F32, tag="wide", bufs=4)
+            for t in range(OUT_BLOCKS):
+                acc = psum.tile([P, GROUP_TOKENS], F32, tag="acc")
+                nc.tensor.matmul_mx(
+                    out=acc[:],
+                    lhsT=w_codes[:, t * P : (t + 1) * P].bitcast(FP8X4),
+                    lhsT_scale=w_scales[:, t * P : (t + 1) * P],
+                    rhs=z_codes[g][:].bitcast(FP8X4),
+                    rhs_scale=z_scales[g][:],
+                    start=True,
+                    stop=True,
+                )
+                nc.scalar.activation(out=exp_v[:, t, :], in_=acc[:], func=ACT.Exp, bias=buf_bias[:, t : t + 1])
+                nc.scalar.activation(out=relu_v[:, t, :], in_=acc[:], func=ACT.Relu, bias=buf_bias[:, t : t + 1])
+            exps[g], relus[g] = exp_v, relu_v
+
+        def combine(g):
+            grouped = stage.tile([P, GROUP_TOKENS * PACK], BF16, name="zb_grouped", align_bytes=64)
+            nc.vector.scalar_tensor_tensor(
+                out=grouped[:].rearrange("q (r t) -> q r t", t=PACK),
+                in0=exps[g][:].rearrange("q t r -> q r t"),
+                scalar=-1.0,
+                in1=relus[g][:].rearrange("q t r -> q r t"),
+                op0=ALU.add,
+                op1=ALU.min,
+            )
+            zb_grouped[g] = grouped
+
+        def quantise_into(codes, scales, g, grouped):
+            cols = slice(g * GROUP_TOKENS, (g + 1) * GROUP_TOKENS)
+            nc.vector.quantize_mx(out=codes[:, cols].bitcast(FP8X4), scales=scales[:, cols], in_=grouped[:])
+
+        p_biased, q_banks, q_last = {}, {}, {}
+
+        def project(codes, scales, weight, bt, half):
+            bank = psum.tile([P, HALF, HID], F32, name="proj", tag=("bank", "acc")[bt % 2])
+            for s in range(HALF):
+                first = (bt * SLOTS + half * HALF + s) * P
+                nc.tensor.matmul_mx(
+                    out=bank[:, s, :],
+                    lhsT=codes[:, first : first + P].bitcast(FP8X4),
+                    lhsT_scale=scales[:, first : first + P],
+                    rhs=l_codes[:, weight * HID : (weight + 1) * HID].bitcast(FP8X4),
+                    rhs_scale=l_scales[:, weight * HID : (weight + 1) * HID],
+                    start=True,
+                    stop=True,
+                )
+            return bank
+
+        def project_tile(bt):
+            p_sb = stage.tile([P, SLOTS, HID], F32, name="p_sb")
+            for half in range(2):
+                p_bank = project(c_codes, c_scales, 0, bt, half)
+                nc.vector.tensor_tensor(
+                    out=p_sb[:, half * HALF : (half + 1) * HALF, :],
+                    in0=p_bank[:],
+                    in1=lam_bias[:].unsqueeze(1).to_broadcast([P, HALF, HID]),
+                    op=ALU.add,
+                )
+            p_biased[bt] = p_sb
+            q_banks[bt] = [project(zb_codes, zb_scales, 1, bt, half) for half in range(2)]
+            q_sb = stage.tile([P, POOL_SLOTS, HID], F32, name="q_sb")
+            nc.scalar.copy(out=q_sb[:], in_=q_banks[bt][1][:, HALF - POOL_SLOTS : HALF, :])
+            q_last[bt] = q_sb
+
+        def pair_chunk(c):
+            bt, part = divmod(c, TILE_CHUNKS)
+            rows = slice(part * CHUNK_ROWS, (part + 1) * CHUNK_ROWS)
+            chunk = stage.tile([P, CHUNK_ROWS, SLOTS, HID], F32, tag="wide", bufs=4)
+
+            def p_over(width):
+                return p_biased[bt][:, rows, :].unsqueeze(2).to_broadcast([P, CHUNK_ROWS, width, HID])
+
+            def q_over(q_part, width):
+                return q_part.unsqueeze(1).to_broadcast([P, CHUNK_ROWS, width, HID])
+
+            rest = HALF - POOL_SLOTS
+            nc.gpsimd.tensor_tensor(
+                out=chunk[:, :, SLOTS - POOL_SLOTS : SLOTS, :],
+                in0=p_over(POOL_SLOTS),
+                in1=q_over(q_last[bt][:], POOL_SLOTS),
+                op=ALU.add,
+            )
+            nc.vector.tensor_tensor(
+                out=chunk[:, :, 0:HALF, :], in0=p_over(HALF), in1=q_over(q_banks[bt][0][:], HALF), op=ALU.add
+            )
+            nc.vector.tensor_tensor(
+                out=chunk[:, :, HALF : HALF + rest, :],
+                in0=p_over(rest),
+                in1=q_over(q_banks[bt][1][:, 0:rest, :], rest),
+                op=ALU.add,
+            )
+            nc.scalar.activation(out=chunk[:], in_=chunk[:], func=ACT.Gelu)
+            nc.sync.dma_start(
+                out=out[bt * P : (bt + 1) * P, rows].rearrange("b i j h -> b (i j h)"),
+                in_=chunk[:].rearrange("b i j h -> b (i j h)"),
+            )
+
+        w_grouped = keep.tile([P, BUF * PACK], BF16, align_bytes=64)
+        nc.vector.tensor_copy(
+            out=w_grouped[:].rearrange("q (o u e) -> q o u e", u=2, e=2),
+            in_=w_raw[:].rearrange("q (e u) o -> q o u e", e=2),
+        )
+        sort_z(0)
+        nc.vector.quantize_mx(out=w_codes[:].bitcast(FP8X4), scales=w_scales[:], in_=w_grouped[:])
+        bias_cols = psum.tile([P, P], BF16, tag="bank")
+        nc.tensor.transpose(out=bias_cols[:], in_=bias_rows[:], identity=ident_bf16[:])
+        nc.vector.tensor_copy(out=buf_bias[:], in_=bias_cols[:, 0:OUT_BLOCKS])
+        l_grouped = keep.tile([P, 2 * HID * PACK], BF16, align_bytes=64)
+        nc.scalar.copy(
+            out=l_grouped[:].rearrange("q (w h t) -> q w h t", w=2, t=PACK),
+            in_=l_raw[:].rearrange("q w t h -> q w h t"),
+        )
+
+        def step(k):
+            if live(k - 1):
+                combine(k - 1)
+            if live(k):
+                buffer_layer(k)
+            if live(k + 1):
+                z_grouped[k + 1] = flip_and_interleave(z_sorted[k + 1], nc.vector.tensor_copy, "z_grouped")
+            if live(k - 1):
+                quantise_into(zb_codes, zb_scales, k - 1, zb_grouped[k - 1])
+            if live(k + 1):
+                bt, half = divmod(k + 1, 2)
+                c_words = c_raw[bt][:].bitcast(F32)[:, half * GROUP_SLOTS * WORDS : (half + 1) * GROUP_SLOTS * WORDS]
+                c_grouped[k + 1] = flip_and_interleave(c_words, nc.scalar.copy, "c_grouped")
+            if live(k + 2):
+                sort_z(k + 2)
+            if live(k + 1):
+                quantise_z(k + 1)
+            if live(k):
+                quantise_into(c_codes, c_scales, k, c_grouped[k])
+            first_chunk = (k - FIRST_CHUNK_STEP) * STEP_CHUNKS
+            next_chunk = first_chunk + STEP_CHUNKS
+            if 0 <= next_chunk < CHUNKS and next_chunk % TILE_CHUNKS == 0:
+                project_tile(next_chunk // TILE_CHUNKS)
+            if first_chunk >= 0:
+                for c in range(first_chunk, next_chunk):
+                    pair_chunk(c)
+
+        step(-1)
+        nc.vector.quantize_mx(out=l_codes[:].bitcast(FP8X4), scales=l_scales[:], in_=l_grouped[:])
+        for k in range(LAST_STEP + 1):
+            step(k)

@@ -99,9 +99,7 @@ def tile_interaction_net_pa_t_kernel(tc, z, cells, buf_W, buf_b, lam_W1, lam_b1,
             )
             z_sorted[g] = words[:]
 
-        def flip_and_interleave(words, copy, name):
-            grouped = stage.tile([P, GROUP_TOKENS * PACK], BF16, name=name, align_bytes=64)
-            pairs = grouped[:].bitcast(F32).rearrange("q (n b u) -> q n b u", n=GROUP_SLOTS, u=2)
+        def flip(words):
             banks = []
             for pair in range(2):
                 bank = psum.tile([P, 2, 2, P], F32, tag="bank")
@@ -112,8 +110,17 @@ def tile_interaction_net_pa_t_kernel(tc, z, cells, buf_W, buf_b, lam_W1, lam_b1,
                             out=bank[:, n, u, :], in_=words[:, first : first + P], identity=ident_f32[:]
                         )
                 banks.append(bank)
+            return banks
+
+        def interleave(copy, banks, grouped, pair):
+            pairs = grouped[:].bitcast(F32).rearrange("q (n b u) -> q n b u", n=GROUP_SLOTS, u=2)
+            copy(out=pairs[:, 2 * pair : 2 * pair + 2], in_=banks[pair][:].rearrange("q n u b -> q n b u"))
+
+        def flip_and_interleave(words, copy, name):
+            grouped = stage.tile([P, GROUP_TOKENS * PACK], BF16, name=name, align_bytes=64)
+            banks = flip(words)
             for pair in range(2):
-                copy(out=pairs[:, 2 * pair : 2 * pair + 2], in_=banks[pair][:].rearrange("q n u b -> q n b u"))
+                interleave(copy, banks, grouped, pair)
             return grouped
 
         def quantise_z(g):
@@ -122,11 +129,15 @@ def tile_interaction_net_pa_t_kernel(tc, z, cells, buf_W, buf_b, lam_W1, lam_b1,
             nc.vector.quantize_mx(out=codes[:].bitcast(FP8X4), scales=scales[:], in_=z_grouped[g][:])
             z_codes[g], z_scales[g] = codes, scales
 
-        def buffer_layer(g):
-            exp_v = stage.tile([P, OUT_BLOCKS, GROUP_TOKENS], F32, tag="wide", bufs=4)
-            relu_v = stage.tile([P, OUT_BLOCKS, GROUP_TOKENS], F32, tag="wide", bufs=4)
+        accs = {}
+
+        def multiply(g):
+            exps[g] = stage.tile([P, OUT_BLOCKS, GROUP_TOKENS], F32, name="exp_v", tag="wide", bufs=4)
+            relus[g] = stage.tile([P, OUT_BLOCKS, GROUP_TOKENS], F32, name="relu_v", tag="wide", bufs=4)
+            accs[g] = []
             for t in range(OUT_BLOCKS):
                 acc = psum.tile([P, GROUP_TOKENS], F32, tag="acc")
+                accs[g].append(acc)
                 nc.tensor.matmul_mx(
                     out=acc[:],
                     lhsT=w_codes[:, t * P : (t + 1) * P].bitcast(FP8X4),
@@ -136,9 +147,10 @@ def tile_interaction_net_pa_t_kernel(tc, z, cells, buf_W, buf_b, lam_W1, lam_b1,
                     start=True,
                     stop=True,
                 )
-                nc.scalar.activation(out=exp_v[:, t, :], in_=acc[:], func=ACT.Exp, bias=buf_bias[:, t : t + 1])
-                nc.scalar.activation(out=relu_v[:, t, :], in_=acc[:], func=ACT.Relu, bias=buf_bias[:, t : t + 1])
-            exps[g], relus[g] = exp_v, relu_v
+
+        def exp_relu(g, t):
+            nc.scalar.activation(out=exps[g][:, t, :], in_=accs[g][t][:], func=ACT.Exp, bias=buf_bias[:, t : t + 1])
+            nc.scalar.activation(out=relus[g][:, t, :], in_=accs[g][t][:], func=ACT.Relu, bias=buf_bias[:, t : t + 1])
 
         def combine(g):
             grouped = stage.tile([P, GROUP_TOKENS * PACK], BF16, name="zb_grouped", align_bytes=64)
@@ -242,9 +254,17 @@ def tile_interaction_net_pa_t_kernel(tc, z, cells, buf_W, buf_b, lam_W1, lam_b1,
             if live(k - 1):
                 combine(k - 1)
             if live(k):
-                buffer_layer(k)
+                multiply(k)
+                exp_relu(k, 0)
+                exp_relu(k, 1)
             if live(k + 1):
-                z_grouped[k + 1] = flip_and_interleave(z_sorted[k + 1], nc.vector.tensor_copy, "z_grouped")
+                z_grouped[k + 1] = stage.tile([P, GROUP_TOKENS * PACK], BF16, name="z_grouped", align_bytes=64)
+                z_banks = flip(z_sorted[k + 1])
+                interleave(nc.vector.tensor_copy, z_banks, z_grouped[k + 1], 0)
+                interleave(nc.scalar.copy, z_banks, z_grouped[k + 1], 1)
+            if live(k):
+                exp_relu(k, 2)
+                exp_relu(k, 3)
             if live(k - 1):
                 quantise_into(zb_codes, zb_scales, k - 1, zb_grouped[k - 1])
             if live(k + 1):

@@ -58,9 +58,8 @@ def tile_interaction_net_pa_t_kernel(tc, z, cells, buf_W, buf_b, lam_W1, lam_b1,
         nc.vector.memset(bias_rows[:], 0.0)
         w_raw = keep.tile([P, PACK, BUF], BF16)
         w_rows = buf_W.rearrange("(d2 t fl) o -> fl d2 t o", t=PACK, fl=4)
-        for fl in range(4):
-            nc.sync.dma_start(out=w_raw[fl:P:4, :, :], in_=w_rows[fl])
-        z_raw = [keep.tile([P, SLOTS * K], BF16, name="z_raw%d" % bt) for bt in range(B_TILES)]
+        z_first = [keep.tile([P, GROUP_SLOTS * K], BF16, name="z_first%d" % g) for g in range(2)]
+        z_raw = [None] + [keep.tile([P, SLOTS * K], BF16, name="z_raw%d" % bt) for bt in range(1, B_TILES)]
         c_raw = [keep.tile([P, SLOTS * K], BF16, name="c_raw%d" % bt) for bt in range(B_TILES)]
         l_raw = keep.tile([P, 2, PACK, HID], BF16)
 
@@ -69,13 +68,30 @@ def tile_interaction_net_pa_t_kernel(tc, z, cells, buf_W, buf_b, lam_W1, lam_b1,
             nc.sync.dma_start(out=z_raw[bt][:], in_=z[rows].rearrange("b f n d -> b (f n d)"))
             nc.sync.dma_start(out=c_raw[bt][:], in_=cells[rows].rearrange("b n k -> b (n k)"))
 
+        def load_first(g):
+            slots = slice(g * GROUP_SLOTS, (g + 1) * GROUP_SLOTS)
+            nc.sync.dma_start(
+                out=z_first[g][:].rearrange("b (f n d) -> b f n d", f=FRAMES, n=GROUP_SLOTS), in_=z[0:P, :, slots, :]
+            )
+
+        def load_first_cells(g):
+            slots = slice(g * GROUP_SLOTS, (g + 1) * GROUP_SLOTS)
+            nc.sync.dma_start(
+                out=c_raw[0][:, g * GROUP_SLOTS * K : (g + 1) * GROUP_SLOTS * K], in_=cells[0:P, slots].rearrange("b n k -> b (n k)")
+            )
+
+        load_first(0)
+        for fl in range(4):
+            nc.sync.dma_start(out=w_raw[fl:P:4, :, :], in_=w_rows[fl])
         nc.sync.dma_start(out=bias_rows[0:OUT_BLOCKS, :], in_=buf_b.rearrange("(t q) -> t q", q=P))
-        load_tile(0)
         nc.sync.dma_start(
             out=l_raw[:, 0].rearrange("q (u e) h -> q u (e h)", u=2),
             in_=lam_W1[0:K, :].rearrange("(u q e) h -> q u (e h)", u=2, e=2),
         )
         nc.sync.dma_start(out=l_raw[:, 1], in_=lam_W1[K : 2 * K, :].rearrange("(t q) h -> q t h", t=PACK))
+        load_first_cells(0)
+        load_first(1)
+        load_first_cells(1)
         nc.sync.dma_start(out=lam_bias[:], in_=lam_b1.partition_broadcast(P))
         for bt in range(1, B_TILES):
             load_tile(bt)
@@ -92,11 +108,12 @@ def tile_interaction_net_pa_t_kernel(tc, z, cells, buf_W, buf_b, lam_W1, lam_b1,
         def sort_z(g):
             bt, half = divmod(g, 2)
             words = stage.tile([P, GROUP_SLOTS * WORDS], F32, name="z_sorted")
-            source = z_raw[bt][:].bitcast(F32).rearrange("b (u fl n d2) -> b n u d2 fl", u=2, fl=4, n=SLOTS)
-            nc.vector.tensor_copy(
-                out=words[:].rearrange("b (n u d2 fl) -> b n u d2 fl", n=GROUP_SLOTS, u=2, fl=4),
-                in_=source[:, half * GROUP_SLOTS : (half + 1) * GROUP_SLOTS],
-            )
+            if bt == 0:
+                source = z_first[g][:].bitcast(F32).rearrange("b (u fl n d2) -> b n u d2 fl", u=2, fl=4, n=GROUP_SLOTS)
+            else:
+                whole = z_raw[bt][:].bitcast(F32).rearrange("b (u fl n d2) -> b n u d2 fl", u=2, fl=4, n=SLOTS)
+                source = whole[:, half * GROUP_SLOTS : (half + 1) * GROUP_SLOTS]
+            nc.vector.tensor_copy(out=words[:].rearrange("b (n u d2 fl) -> b n u d2 fl", n=GROUP_SLOTS, u=2, fl=4), in_=source)
             z_sorted[g] = words[:]
 
         def flip(words):
@@ -234,21 +251,28 @@ def tile_interaction_net_pa_t_kernel(tc, z, cells, buf_W, buf_b, lam_W1, lam_b1,
                 in_=chunk[:].rearrange("b i j h -> b (i j h)"),
             )
 
+        sort_z(0)
         w_grouped = keep.tile([P, BUF * PACK], BF16, align_bytes=64)
         nc.vector.tensor_copy(
             out=w_grouped[:].rearrange("q (o u e) -> q o u e", u=2, e=2),
             in_=w_raw[:].rearrange("q (e u) o -> q o u e", e=2),
         )
-        sort_z(0)
+        z_grouped[0] = stage.tile([P, GROUP_TOKENS * PACK], BF16, name="z_grouped", align_bytes=64)
+        first_banks = flip(z_sorted[0])
+        interleave(nc.vector.tensor_copy, first_banks, z_grouped[0], 0)
+        interleave(nc.scalar.copy, first_banks, z_grouped[0], 1)
         nc.vector.quantize_mx(out=w_codes[:].bitcast(FP8X4), scales=w_scales[:], in_=w_grouped[:])
         bias_cols = psum.tile([P, P], BF16, tag="bank")
         nc.tensor.transpose(out=bias_cols[:], in_=bias_rows[:], identity=ident_bf16[:])
         nc.vector.tensor_copy(out=buf_bias[:], in_=bias_cols[:, 0:OUT_BLOCKS])
+        quantise_z(0)
         l_grouped = keep.tile([P, 2 * HID * PACK], BF16, align_bytes=64)
         nc.scalar.copy(
             out=l_grouped[:].rearrange("q (w h t) -> q w h t", w=2, t=PACK),
             in_=l_raw[:].rearrange("q w t h -> q w h t"),
         )
+        c_grouped[0] = flip_and_interleave(c_raw[0][:].bitcast(F32)[:, 0 : GROUP_SLOTS * WORDS], nc.scalar.copy, "c_grouped")
+        sort_z(1)
 
         def step(k):
             if live(k - 1):
@@ -285,7 +309,7 @@ def tile_interaction_net_pa_t_kernel(tc, z, cells, buf_W, buf_b, lam_W1, lam_b1,
                 for c in range(first_chunk, next_chunk):
                     pair_chunk(c)
 
-        step(-1)
-        nc.vector.quantize_mx(out=l_codes[:].bitcast(FP8X4), scales=l_scales[:], in_=l_grouped[:])
         for k in range(LAST_STEP + 1):
             step(k)
+            if k == 0:
+                nc.vector.quantize_mx(out=l_codes[:].bitcast(FP8X4), scales=l_scales[:], in_=l_grouped[:])

import concourse.masks as masks
import concourse.mybir as mybir

F32 = mybir.dt.float32
BF16 = mybir.dt.bfloat16
U32 = mybir.dt.uint32
U8 = mybir.dt.uint8
FP8X4 = mybir.dt.float8_e4m3fn_x4
ACT = mybir.ActivationFunctionType
ALU = mybir.AluOpType

P = 128
BATCH, FRAMES, SLOTS, FEAT, HID, CELL, BUF = 512, 8, 8, 64, 128, 512, 512
PACK = 4
K = P * PACK
WORDS = K // 2
B_TILES = BATCH // P
GROUP_SLOTS = 4
GROUP_TOKENS = GROUP_SLOTS * P
GROUPS = B_TILES * SLOTS // GROUP_SLOTS
OUT_BLOCKS = BUF // P
HALF = SLOTS // 2
CHUNK_ROWS = 2
TILE_CHUNKS = SLOTS // CHUNK_ROWS
CHUNKS = B_TILES * TILE_CHUNKS
STEP_CHUNKS = 2
POOL_SLOTS = 2
FIRST_CHUNK_STEP = GROUPS - 1
LAST_STEP = FIRST_CHUNK_STEP + CHUNKS // STEP_CHUNKS - 1

FLOPS = 2 * BATCH * SLOTS * K * (BUF + HID + HID)


def tile_interaction_net_pa_t_kernel(tc, z, cells, buf_W, buf_b, lam_W1, lam_b1, out):
    nc = tc.nc

    def live(g):
        return 0 <= g < GROUPS

    with (
        tc.manual_schedule(),
        tc.tile_pool(name="keep", bufs=1) as keep,
        tc.tile_pool(name="stage", bufs=2) as stage,
        tc.psum_pool(name="psum", bufs=4) as psum,
    ):
        w_codes = keep.tile([P, BUF], U32, align_bytes=64)
        w_scales = keep.tile([P, BUF], U8, align_bytes=64)
        l_codes = keep.tile([P, 2 * HID], U32, align_bytes=64)
        l_scales = keep.tile([P, 2 * HID], U8, align_bytes=64)
        c_codes = keep.tile([P, GROUPS * GROUP_TOKENS], U32, align_bytes=64)
        c_scales = keep.tile([P, GROUPS * GROUP_TOKENS], U8, align_bytes=64)
        zb_codes = keep.tile([P, GROUPS * GROUP_TOKENS], U32, align_bytes=64)
        zb_scales = keep.tile([P, GROUPS * GROUP_TOKENS], U8, align_bytes=64)
        buf_bias = keep.tile([P, OUT_BLOCKS], F32)
        lam_bias = keep.tile([P, HID], BF16)

        bias_rows = keep.tile([P, P], BF16)
        nc.vector.memset(bias_rows[:], 0.0)
        w_raw = keep.tile([P, PACK, BUF], BF16)
        w_rows = buf_W.rearrange("(d2 t fl) o -> fl d2 t o", t=PACK, fl=4)
        z_first = [keep.tile([P, GROUP_SLOTS * K], BF16, name="z_first%d" % g) for g in range(2)]
        z_raw = [None] + [keep.tile([P, SLOTS * K], BF16, name="z_raw%d" % bt) for bt in range(1, B_TILES)]
        c_raw = [keep.tile([P, SLOTS * K], BF16, name="c_raw%d" % bt) for bt in range(B_TILES)]
        l_raw = keep.tile([P, 2, PACK, HID], BF16)

        def load_tile(bt):
            rows = slice(bt * P, (bt + 1) * P)
            nc.sync.dma_start(out=z_raw[bt][:], in_=z[rows].rearrange("b f n d -> b (f n d)"))
            nc.sync.dma_start(out=c_raw[bt][:], in_=cells[rows].rearrange("b n k -> b (n k)"))

        def load_first(g):
            slots = slice(g * GROUP_SLOTS, (g + 1) * GROUP_SLOTS)
            nc.sync.dma_start(
                out=z_first[g][:].rearrange("b (f n d) -> b f n d", f=FRAMES, n=GROUP_SLOTS), in_=z[0:P, :, slots, :]
            )

        def load_first_cells(g):
            slots = slice(g * GROUP_SLOTS, (g + 1) * GROUP_SLOTS)
            nc.sync.dma_start(
                out=c_raw[0][:, g * GROUP_SLOTS * K : (g + 1) * GROUP_SLOTS * K], in_=cells[0:P, slots].rearrange("b n k -> b (n k)")
            )

        load_first(0)
        for fl in range(4):
            nc.sync.dma_start(out=w_raw[fl:P:4, :, :], in_=w_rows[fl])
        nc.sync.dma_start(out=bias_rows[0:OUT_BLOCKS, :], in_=buf_b.rearrange("(t q) -> t q", q=P))
        nc.sync.dma_start(
            out=l_raw[:, 0].rearrange("q (u e) h -> q u (e h)", u=2),
            in_=lam_W1[0:K, :].rearrange("(u q e) h -> q u (e h)", u=2, e=2),
        )
        nc.sync.dma_start(out=l_raw[:, 1], in_=lam_W1[K : 2 * K, :].rearrange("(t q) h -> q t h", t=PACK))
        load_first_cells(0)
        load_first(1)
        load_first_cells(1)
        nc.sync.dma_start(out=lam_bias[:], in_=lam_b1.partition_broadcast(P))
        for bt in range(1, B_TILES):
            load_tile(bt)

        ident_f32 = keep.tile([P, P], F32)
        masks.make_identity(nc, ident_f32[:])
        ident_bf16 = keep.tile([P, P], BF16)
        masks.make_identity(nc, ident_bf16[:])

        z_sorted, z_grouped, z_codes, z_scales = {}, {}, {}, {}
        c_grouped = {}
        exps, relus, zb_grouped = {}, {}, {}

        def sort_z(g):
            bt, half = divmod(g, 2)
            words = stage.tile([P, GROUP_SLOTS * WORDS], F32, name="z_sorted")
            if bt == 0:
                source = z_first[g][:].bitcast(F32).rearrange("b (u fl n d2) -> b n u d2 fl", u=2, fl=4, n=GROUP_SLOTS)
            else:
                whole = z_raw[bt][:].bitcast(F32).rearrange("b (u fl n d2) -> b n u d2 fl", u=2, fl=4, n=SLOTS)
                source = whole[:, half * GROUP_SLOTS : (half + 1) * GROUP_SLOTS]
            nc.vector.tensor_copy(out=words[:].rearrange("b (n u d2 fl) -> b n u d2 fl", n=GROUP_SLOTS, u=2, fl=4), in_=source)
            z_sorted[g] = words[:]

        def flip(words):
            banks = []
            for pair in range(2):
                bank = psum.tile([P, 2, 2, P], F32, tag="bank")
                for n in range(2):
                    for u in range(2):
                        first = ((2 * pair + n) * 2 + u) * P
                        nc.tensor.transpose(
                            out=bank[:, n, u, :], in_=words[:, first : first + P], identity=ident_f32[:]
                        )
                banks.append(bank)
            return banks

        def interleave(copy, banks, grouped, pair):
            pairs = grouped[:].bitcast(F32).rearrange("q (n b u) -> q n b u", n=GROUP_SLOTS, u=2)
            copy(out=pairs[:, 2 * pair : 2 * pair + 2], in_=banks[pair][:].rearrange("q n u b -> q n b u"))

        def flip_and_interleave(words, copy, name):
            grouped = stage.tile([P, GROUP_TOKENS * PACK], BF16, name=name, align_bytes=64)
            banks = flip(words)
            for pair in range(2):
                interleave(copy, banks, grouped, pair)
            return grouped

        def quantise_z(g):
            codes = stage.tile([P, GROUP_TOKENS], U32, name="z_codes", align_bytes=64)
            scales = stage.tile([P, GROUP_TOKENS], U8, name="z_scales", align_bytes=64)
            nc.vector.quantize_mx(out=codes[:].bitcast(FP8X4), scales=scales[:], in_=z_grouped[g][:])
            z_codes[g], z_scales[g] = codes, scales

        accs = {}

        def multiply(g):
            exps[g] = stage.tile([P, OUT_BLOCKS, GROUP_TOKENS], F32, name="exp_v", tag="wide", bufs=4)
            relus[g] = stage.tile([P, OUT_BLOCKS, GROUP_TOKENS], F32, name="relu_v", tag="wide", bufs=4)
            accs[g] = []
            for t in range(OUT_BLOCKS):
                acc = psum.tile([P, GROUP_TOKENS], F32, tag="acc")
                accs[g].append(acc)
                nc.tensor.matmul_mx(
                    out=acc[:],
                    lhsT=w_codes[:, t * P : (t + 1) * P].bitcast(FP8X4),
                    lhsT_scale=w_scales[:, t * P : (t + 1) * P],
                    rhs=z_codes[g][:].bitcast(FP8X4),
                    rhs_scale=z_scales[g][:],
                    start=True,
                    stop=True,
                )

        def exp_relu(g, t):
            nc.scalar.activation(out=exps[g][:, t, :], in_=accs[g][t][:], func=ACT.Exp, bias=buf_bias[:, t : t + 1])
            nc.scalar.activation(out=relus[g][:, t, :], in_=accs[g][t][:], func=ACT.Relu, bias=buf_bias[:, t : t + 1])

        def combine(g):
            grouped = stage.tile([P, GROUP_TOKENS * PACK], BF16, name="zb_grouped", align_bytes=64)
            nc.vector.scalar_tensor_tensor(
                out=grouped[:].rearrange("q (r t) -> q r t", t=PACK),
                in0=exps[g][:].rearrange("q t r -> q r t"),
                scalar=-1.0,
                in1=relus[g][:].rearrange("q t r -> q r t"),
                op0=ALU.add,
                op1=ALU.min,
            )
            zb_grouped[g] = grouped

        def quantise_into(codes, scales, g, grouped):
            cols = slice(g * GROUP_TOKENS, (g + 1) * GROUP_TOKENS)
            nc.vector.quantize_mx(out=codes[:, cols].bitcast(FP8X4), scales=scales[:, cols], in_=grouped[:])

        p_biased, q_banks, q_last = {}, {}, {}

        def project(codes, scales, weight, bt, half):
            bank = psum.tile([P, HALF, HID], F32, name="proj", tag=("bank", "acc")[bt % 2])
            for s in range(HALF):
                first = (bt * SLOTS + half * HALF + s) * P
                nc.tensor.matmul_mx(
                    out=bank[:, s, :],
                    lhsT=codes[:, first : first + P].bitcast(FP8X4),
                    lhsT_scale=scales[:, first : first + P],
                    rhs=l_codes[:, weight * HID : (weight + 1) * HID].bitcast(FP8X4),
                    rhs_scale=l_scales[:, weight * HID : (weight + 1) * HID],
                    start=True,
                    stop=True,
                )
            return bank

        def project_tile(bt):
            p_sb = stage.tile([P, SLOTS, HID], F32, name="p_sb")
            for half in range(2):
                p_bank = project(c_codes, c_scales, 0, bt, half)
                nc.vector.tensor_tensor(
                    out=p_sb[:, half * HALF : (half + 1) * HALF, :],
                    in0=p_bank[:],
                    in1=lam_bias[:].unsqueeze(1).to_broadcast([P, HALF, HID]),
                    op=ALU.add,
                )
            p_biased[bt] = p_sb
            q_banks[bt] = [project(zb_codes, zb_scales, 1, bt, half) for half in range(2)]
            q_sb = stage.tile([P, POOL_SLOTS, HID], F32, name="q_sb")
            nc.scalar.copy(out=q_sb[:], in_=q_banks[bt][1][:, HALF - POOL_SLOTS : HALF, :])
            q_last[bt] = q_sb

        def pair_chunk(c):
            bt, part = divmod(c, TILE_CHUNKS)
            rows = slice(part * CHUNK_ROWS, (part + 1) * CHUNK_ROWS)
            chunk = stage.tile([P, CHUNK_ROWS, SLOTS, HID], F32, tag="wide", bufs=4)

            def p_over(width):
                return p_biased[bt][:, rows, :].unsqueeze(2).to_broadcast([P, CHUNK_ROWS, width, HID])

            def q_over(q_part, width):
                return q_part.unsqueeze(1).to_broadcast([P, CHUNK_ROWS, width, HID])

            rest = HALF - POOL_SLOTS
            nc.gpsimd.tensor_tensor(
                out=chunk[:, :, SLOTS - POOL_SLOTS : SLOTS, :],
                in0=p_over(POOL_SLOTS),
                in1=q_over(q_last[bt][:], POOL_SLOTS),
                op=ALU.add,
            )
            nc.vector.tensor_tensor(
                out=chunk[:, :, 0:HALF, :], in0=p_over(HALF), in1=q_over(q_banks[bt][0][:], HALF), op=ALU.add
            )
            nc.vector.tensor_tensor(
                out=chunk[:, :, HALF : HALF + rest, :],
                in0=p_over(rest),
                in1=q_over(q_banks[bt][1][:, 0:rest, :], rest),
                op=ALU.add,
            )
            nc.scalar.activation(out=chunk[:], in_=chunk[:], func=ACT.Gelu)
            nc.sync.dma_start(
                out=out[bt * P : (bt + 1) * P, rows].rearrange("b i j h -> b (i j h)"),
                in_=chunk[:].rearrange("b i j h -> b (i j h)"),
            )

        sort_z(0)
        w_grouped = keep.tile([P, BUF * PACK], BF16, align_bytes=64)
        nc.vector.tensor_copy(
            out=w_grouped[:].rearrange("q (o u e) -> q o u e", u=2, e=2),
            in_=w_raw[:].rearrange("q (e u) o -> q o u e", e=2),
        )
        z_grouped[0] = stage.tile([P, GROUP_TOKENS * PACK], BF16, name="z_grouped", align_bytes=64)
        first_banks = flip(z_sorted[0])
        interleave(nc.vector.tensor_copy, first_banks, z_grouped[0], 0)
        interleave(nc.scalar.copy, first_banks, z_grouped[0], 1)
        nc.vector.quantize_mx(out=w_codes[:].bitcast(FP8X4), scales=w_scales[:], in_=w_grouped[:])
        bias_cols = psum.tile([P, P], BF16, tag="bank")
        nc.tensor.transpose(out=bias_cols[:], in_=bias_rows[:], identity=ident_bf16[:])
        nc.vector.tensor_copy(out=buf_bias[:], in_=bias_cols[:, 0:OUT_BLOCKS])
        quantise_z(0)
        l_grouped = keep.tile([P, 2 * HID * PACK], BF16, align_bytes=64)
        nc.scalar.copy(
            out=l_grouped[:].rearrange("q (w h t) -> q w h t", w=2, t=PACK),
            in_=l_raw[:].rearrange("q w t h -> q w h t"),
        )
        c_grouped[0] = flip_and_interleave(c_raw[0][:].bitcast(F32)[:, 0 : GROUP_SLOTS * WORDS], nc.scalar.copy, "c_grouped")
        sort_z(1)

        def step(k):
            if live(k - 1):
                combine(k - 1)
            if live(k):
                multiply(k)
                exp_relu(k, 0)
                exp_relu(k, 1)
            if live(k + 1):
                z_grouped[k + 1] = stage.tile([P, GROUP_TOKENS * PACK], BF16, name="z_grouped", align_bytes=64)
                z_banks = flip(z_sorted[k + 1])
                interleave(nc.vector.tensor_copy, z_banks, z_grouped[k + 1], 0)
                interleave(nc.scalar.copy, z_banks, z_grouped[k + 1], 1)
            if live(k):
                exp_relu(k, 2)
                exp_relu(k, 3)
            if live(k - 1):
                quantise_into(zb_codes, zb_scales, k - 1, zb_grouped[k - 1])
            if live(k + 1):
                bt, half = divmod(k + 1, 2)
                c_words = c_raw[bt][:].bitcast(F32)[:, half * GROUP_SLOTS * WORDS : (half + 1) * GROUP_SLOTS * WORDS]
                c_grouped[k + 1] = flip_and_interleave(c_words, nc.scalar.copy, "c_grouped")
            if live(k + 2):
                sort_z(k + 2)
            if live(k + 1):
                quantise_z(k + 1)
            if live(k):
                quantise_into(c_codes, c_scales, k, c_grouped[k])
            first_chunk = (k - FIRST_CHUNK_STEP) * STEP_CHUNKS
            next_chunk = first_chunk + STEP_CHUNKS
            if 0 <= next_chunk < CHUNKS and next_chunk % TILE_CHUNKS == 0:
                project_tile(next_chunk // TILE_CHUNKS)
            if first_chunk >= 0:
                for c in range(first_chunk, next_chunk):
                    pair_chunk(c)

        for k in range(LAST_STEP + 1):
            step(k)
            if k == 0:
                nc.vector.quantize_mx(out=l_codes[:].bitcast(FP8X4), scales=l_scales[:], in_=l_grouped[:])
